import numpy as np
import ml_dtypes


def mxq(x, axis, fmt="e4m3"):
    dtype, down = {"e4m3": (ml_dtypes.float8_e4m3fn, 7), "e5m2": (ml_dtypes.float8_e5m2, 14)}[fmt]
    v = np.moveaxis(np.asarray(x, np.float32).astype(ml_dtypes.bfloat16).astype(np.float64), axis, -1)
    blocks = v.reshape(v.shape[:-1] + (-1, 32))
    amax = np.abs(blocks).max(-1, keepdims=True)
    byte = np.maximum(np.where(amax > 0, np.frexp(amax)[1] - 1 + 127, 0) - down, 1)
    scale = np.exp2(byte - 127.0)
    codes = (blocks / scale).astype(np.float32).astype(dtype).astype(np.float64)
    return np.moveaxis((codes * scale).reshape(v.shape), -1, axis)


WIDE = False


def mx_kscale(k):
    if not WIDE:
        return np.ones(k)
    levels = np.array([10, -10, 5, -5, 0])
    if k % 512:
        return np.exp2(np.random.permutation(np.resize(levels, k // 32))).repeat(32)
    a = np.empty((k // 512, 16))
    for p in range(k // 512):
        a[p, :8] = np.random.permutation(np.resize(levels, 8))
        for g in range(8):
            far = levels[np.abs(levels - a[p, g]) >= 10]
            a[p, g + 8] = far[np.random.randint(len(far))]
    return np.exp2(a.ravel()).repeat(32)


BF16 = ml_dtypes.bfloat16


def bf(x):
    return np.asarray(x, np.float32).astype(BF16)


def f64(x):
    return np.asarray(x).astype(np.float64)


E2M1 = np.array([0.0, 0.5, 1.0, 1.5, 2.0, 3.0, 4.0, 6.0, -0.0, -0.5, -1.0, -1.5, -2.0, -3.0, -4.0, -6.0])


def pack_weight(w, fmt):
    k, n = w.shape
    w = f64(bf(w)).reshape(k // 32, 32, n)
    amax = np.abs(w).max(1)
    if fmt == "e4m3":
        byte = np.frexp(amax)[1] - 1 + 127 - 7
    else:
        mant, ex = np.frexp(amax / 6.0)
        byte = np.where(mant > 0.5, ex, ex - 1) + 127
    byte = np.clip(np.where(amax > 0, byte, 1), 1, 254)
    scaled = (w * np.exp2(127.0 - byte)[:, None, :]).reshape(k, n).astype(np.float32)
    by_word = np.ascontiguousarray(scaled.reshape(k // 512, 128, 4, n).transpose(0, 1, 3, 2))
    if fmt == "e4m3":
        words = by_word.astype(ml_dtypes.float8_e4m3fn).view(np.uint8)
    else:
        c = by_word.astype(ml_dtypes.float4_e2m1fn).view(np.uint8) & 0xF
        words = c[..., 0::2] | (c[..., 1::2] << 4)
    return np.ascontiguousarray(words), np.ascontiguousarray(byte.astype(np.uint8).reshape(k // 512, 16, n))


def unpack_weight(words, scales, fmt):
    g, p, n, _ = words.shape
    if fmt == "e4m3":
        vals = np.ascontiguousarray(words).view(ml_dtypes.float8_e4m3fn).astype(np.float64)
    else:
        nib = np.empty((g, p, n, 4), np.uint8)
        nib[..., 0::2] = words & 0xF
        nib[..., 1::2] = words >> 4
        vals = E2M1[nib]
    vals = vals * np.repeat(np.exp2(scales.astype(np.float64) - 127.0), 8, axis=1)[..., None]
    return vals.transpose(0, 1, 3, 2).reshape(g * 512, n)


B, NR, NQ, D, H, F = 4, 1024, 2048, 2, 256, 512
C = H + H
LN_EPS = 1e-5


def draw0():
    s, t = mx_kscale(C), mx_kscale(F)
    pq = bf(np.random.standard_normal((B, NQ, H)) * s[:H])
    attended = bf(np.random.standard_normal((B, NQ, H)) * s[H:])
    Wf1_words, Wf1_scales = pack_weight(np.random.standard_normal((C, F)) / np.sqrt(C) / s[:, None] * t, "e4m3")
    bf1 = bf(np.random.standard_normal(F) * 0.2 * t)
    Wf2_words, Wf2_scales = pack_weight(np.random.standard_normal((F, H)) * 1.5 / np.sqrt(F) / t[:, None], "e4m3")
    return {"pq": pq,
            "attended": attended,
            "Wf1_words": Wf1_words,
            "Wf1_scales": Wf1_scales,
            "bf1": bf1,
            "Wf2_words": Wf2_words,
            "Wf2_scales": Wf2_scales,
            "bf2": bf(np.random.standard_normal(H) * 0.3),
            "ln_g": bf(1.0 + 0.1 * np.random.standard_normal(H)),
            "ln_b": bf(0.1 * np.random.standard_normal(H))}


def core(pq, attended, Wf1_words, Wf1_scales, bf1, Wf2_words, Wf2_scales, bf2, ln_g, ln_b):
    final_inp = np.concatenate([f64(pq), f64(attended)], axis=2)
    h = np.maximum((mxq(final_inp, 2, "e4m3") @ unpack_weight(Wf1_words, Wf1_scales, "e4m3")) + f64(bf1), 0.0)
    y = (mxq(h, 2, "e4m3") @ unpack_weight(Wf2_words, Wf2_scales, "e4m3")) + f64(bf2)
    mu = np.mean(y, axis=-1, keepdims=True)
    var = np.mean(np.square(y - mu), axis=-1, keepdims=True)
    return (y - mu) / np.sqrt(var + LN_EPS) * f64(ln_g) + f64(ln_b)


def e4m3fn_bytes(y):
    return np.clip(np.asarray(y, np.float64), -448.0, 448.0).astype(np.float32).astype(ml_dtypes.float8_e4m3fn).view(np.uint8)


def e4m3fn_values(b):
    return np.asarray(b, np.uint8).view(ml_dtypes.float8_e4m3fn).astype(np.float64)


def setup_inputs():
    d = draw0()
    x0 = np.asarray(d['pq']).astype(np.float64)
    s = (np.max(np.abs(x0), axis=(0, 1), keepdims=True) / 448.0).astype(np.float32)
    out = {}
    for k, v in d.items():
        if k == 'pq':
            out['pq_bytes'] = e4m3fn_bytes(x0 / s.astype(np.float64))
            out['pq_scale'] = s
        else:
            out[k] = v
    return out


def reference(pq_bytes, pq_scale, attended, Wf1_words, Wf1_scales, bf1, Wf2_words, Wf2_scales, bf2, ln_g, ln_b):
    return core(e4m3fn_values(pq_bytes) * pq_scale.astype(np.float64), attended, Wf1_words, Wf1_scales, bf1, Wf2_words, Wf2_scales, bf2, ln_g, ln_b)

@@ -1,0 +1,285 @@
+from contextlib import ExitStack
+
+import concourse.mybir as mybir
+from concourse.masks import make_identity
+
+F32 = mybir.dt.float32
+BF16 = mybir.dt.bfloat16
+I32 = mybir.dt.int32
+U32 = mybir.dt.uint32
+U8 = mybir.dt.uint8
+FP8 = mybir.dt.float8_e4m3fn
+FP8X4 = mybir.dt.float8_e4m3fn_x4
+ALU = mybir.AluOpType
+ACT = mybir.ActivationFunctionType
+
+P = 128
+H = 256
+C = 512
+F = 512
+TOKENS = 8192
+TILES = 4
+GROUP = P * TILES
+GROUPS = TOKENS // GROUP
+EPS = 1e-5
+FLOPS = 2 * TOKENS * C * F + 2 * TOKENS * F * H
+
+S_TOKENS = 320
+
+
+def tile_spatialattentionlayer_pb_t_w8_kernel(
+    tc, pq_bytes, pq_scale, attended, w1_words, w1_scales, bf1, w2_words, w2_scales, bf2, ln_g, ln_b, out
+):
+    nc = tc.nc
+    with ExitStack() as ctx:
+        keep = ctx.enter_context(tc.tile_pool(name="keep", bufs=1))
+        inputs = ctx.enter_context(tc.tile_pool(name="inputs", bufs=1))
+        work = ctx.enter_context(tc.tile_pool(name="work", bufs=3))
+        psum_c = ctx.enter_context(tc.psum_pool(name="psum_c", bufs=2))
+        psum_h = ctx.enter_context(tc.psum_pool(name="psum_h", bufs=4))
+        psum_y = ctx.enter_context(tc.psum_pool(name="psum_y", bufs=2))
+        ctx.enter_context(tc.manual_schedule())
+
+        pq_rows = pq_bytes.rearrange("b n c -> (b n) c").rearrange("(s p j) c -> s p (j c)", p=P, j=2 * TILES)
+        att_rows = attended.rearrange("b n c -> (b n) c").rearrange("(s p k j) c -> s k p j c", p=P, k=2, j=TILES)
+        out_rows = out.rearrange("b n c -> (b n) c").rearrange("(s p k j) c -> s k p (j c)", p=P, k=2, j=TILES)
+
+        scale_row = keep.tile([P, H], F32, name="scale_row")
+        bias1_bf = keep.tile([P, 4], BF16, name="bias1_bf")
+        bias1 = keep.tile([P, 4], F32, name="bias1")
+        bias2 = keep.tile([P, H], BF16, name="bias2")
+        gain = keep.tile([P, H], BF16, name="gain")
+        shift = keep.tile([P, H], BF16, name="shift")
+        ident = keep.tile([P, P], F32, name="ident")
+        neg_half = keep.tile([P, TILES], F32, name="neg_half")
+        warm = keep.tile([P, 1], F32, name="warm")
+        w1_in = keep.tile([P, F], U32, name="w1_in", align_bytes=64)
+        w1 = keep.tile([P, F], U32, name="w1", align_bytes=64)
+        w1_sc_in = keep.tile([P, F], U8, name="w1_sc_in", align_bytes=64)
+        w1_sc = keep.tile([P, F], U8, name="w1_sc", align_bytes=64)
+        w2 = keep.tile([P, H], U32, name="w2", align_bytes=64)
+        w2_sc = keep.tile([P, H], U8, name="w2_sc", align_bytes=64)
+
+        codes_in = [inputs.tile([P, 2 * TILES * H], U8, name="pq%d" % s) for s in range(GROUPS // 2)]
+        c_in = [inputs.tile([P, TILES, C], BF16, name="c%d" % g) for g in range(GROUPS)]
+
+        def load_pq(s):
+            nc.sync.dma_start(out=codes_in[s][:], in_=pq_rows[s])
+
+        def load_att(g):
+            nc.sync.dma_start(out=c_in[g][:, :, H:C], in_=att_rows[g // 2, g % 2])
+
+        nc.vector.memset(w1_sc_in[:].bitcast(I32), 0)
+        nc.vector.memset(w2_sc[:].bitcast(I32), 0)
+        nc.vector.memset(warm[:], 0.0)
+        nc.gpsimd.memset(neg_half[:], -0.5)
+        make_identity(nc, ident[:])
+        nc.scalar.activation(out=warm[:], in_=warm[:], func=ACT.Relu)
+
+        nc.sync.dma_start(out=scale_row[:], in_=pq_scale.rearrange("a b c -> (a b c)").partition_broadcast(P))
+        load_pq(0)
+        load_att(0)
+        nc.sync.dma_start(out=w1_in[:].bitcast(I32), in_=w1_words[0].rearrange("p n t -> p (n t)").bitcast(I32))
+        for q in range(4):
+            nc.sync.dma_start(
+                out=w1_sc_in[32 * q : 32 * q + 4, :].bitcast(I32), in_=w1_scales[0, 4 * q : 4 * q + 4, :].bitcast(I32)
+            )
+        for q in range(4):
+            nc.sync.dma_start(
+                out=w2_sc[32 * q : 32 * q + 4, :].bitcast(I32), in_=w2_scales[0, 4 * q : 4 * q + 4, :].bitcast(I32)
+            )
+        nc.sync.dma_start(out=bias1_bf[:], in_=bf1.rearrange("(p t) -> p t", t=4))
+        load_att(1)
+        nc.sync.dma_start(out=w2[:].bitcast(I32), in_=w2_words[0].rearrange("p n t -> p (n t)").bitcast(I32))
+        nc.sync.dma_start(out=bias2[:], in_=bf2.partition_broadcast(P))
+        nc.sync.dma_start(out=gain[:], in_=ln_g.partition_broadcast(P))
+        nc.sync.dma_start(out=shift[:], in_=ln_b.partition_broadcast(P))
+        for s in range(1, GROUPS // 2):
+            load_pq(s)
+            load_att(2 * s)
+            load_att(2 * s + 1)
+
+        def product(g):
+            for j in range(TILES):
+                base = (g % 2 * TILES + j) * H
+                nc.vector.tensor_tensor(
+                    out=c_in[g][:, j, 0:H],
+                    in0=codes_in[g // 2][:, base : base + H].bitcast(FP8),
+                    in1=scale_row[:],
+                    op=ALU.mult,
+                )
+
+        turned = {}
+        c_mx = {}
+        h_psum = {}
+        h_flat = {}
+        h_mx = {}
+        y_psum = {}
+        y_rows = {}
+        sums = {}
+        squares = {}
+        stats = {}
+
+        def turn(g):
+            words = c_in[g][:].bitcast(F32)
+            for half in range(2):
+                ct = psum_c.tile([P, 2, 2, P], F32, name="ct")
+                for jj in range(2):
+                    for u in range(2):
+                        nc.tensor.transpose(ct[:, jj, u, :], words[:, 2 * half + jj, u : C // 2 : 2], ident[:])
+                turned[g, half] = ct
+
+        c_grouped = {}
+
+        def empty_turned(g):
+            grouped = work.tile([P, GROUP * 4], BF16, name="c_grouped", align_bytes=64)
+            for half in range(2):
+                nc.scalar.copy(
+                    out=grouped[:, half * 1024 : half * 1024 + 1024].bitcast(F32).rearrange("p (j r u) -> p j r u", j=2, u=2),
+                    in_=turned.pop((g, half))[:].rearrange("p j u r -> p j r u"),
+                )
+            c_grouped[g] = grouped
+
+        def quantize(grouped, name):
+            codes = work.tile([P, GROUP], U32, name=name + "_codes", align_bytes=64)
+            scales = work.tile([P, GROUP], U8, name=name + "_scales", align_bytes=64)
+            nc.vector.quantize_mx(out=codes[:].bitcast(FP8X4), scales=scales[:], in_=grouped[:])
+            return codes, scales
+
+        def quantize_c(g):
+            c_mx[g] = quantize(c_grouped.pop(g), "c")
+
+        def layer1(g):
+            codes, scales = c_mx.pop(g)
+            h_psum[g] = []
+            for t in range(4):
+                hp = psum_h.tile([P, GROUP], F32, name="hp")
+                nc.tensor.matmul_mx(
+                    out=hp[:],
+                    lhsT=w1[:, t * P : t * P + P].bitcast(FP8X4),
+                    lhsT_scale=w1_sc[:, t * P : t * P + P],
+                    rhs=codes[:].bitcast(FP8X4),
+                    rhs_scale=scales[:],
+                    start=True,
+                    stop=True,
+                )
+                h_psum[g].append(hp)
+
+        def hidden(g):
+            planes = work.tile([P, 4, GROUP], BF16, name="h_flat")
+            for t in range(4):
+                nc.scalar.activation(out=planes[:, t, :], in_=h_psum[g][t][:], func=ACT.Relu, bias=bias1[:, t : t + 1])
+            h_flat[g] = planes
+
+        h_grouped = {}
+
+        def interleave_views(g, lo, hi):
+            if g not in h_grouped:
+                h_grouped[g] = work.tile([P, GROUP * 4], BF16, name="h_grouped", align_bytes=64)
+            dst = h_grouped[g][:, lo * 4 : hi * 4].rearrange("p (c i t) -> p c t i", i=4, t=4)
+            src = h_flat[g][:, :, lo:hi].rearrange("p t (c i) -> p c t i", i=4)
+            return dst, src
+
+        def interleave_s(g):
+            dst, src = interleave_views(g, 0, S_TOKENS)
+            nc.scalar.copy(out=dst, in_=src)
+
+        def interleave_v(g):
+            dst, src = interleave_views(g, S_TOKENS, GROUP)
+            nc.vector.tensor_copy(out=dst, in_=src)
+
+        def quantize_h(g):
+            h_mx[g] = quantize(h_grouped.pop(g), "h")
+
+        def layer2(g):
+            codes, scales = h_mx.pop(g)
+            for half in range(2):
+                yp = psum_y.tile([P, 2, H], F32, name="yp")
+                for jj in range(2):
+                    cols = slice((2 * half + jj) * P, (2 * half + jj + 1) * P)
+                    nc.tensor.matmul_mx(
+                        out=yp[:, jj, :],
+                        lhsT=codes[:, cols].bitcast(FP8X4),
+                        lhsT_scale=scales[:, cols],
+                        rhs=w2[:].bitcast(FP8X4),
+                        rhs_scale=w2_sc[:],
+                        start=True,
+                        stop=True,
+                    )
+                y_psum[g, half] = yp
+
+        def add_bias2(g):
+            y = work.tile([P, TILES, H], F32, name="y")
+            total = work.tile([P, TILES], F32, name="total")
+            for j in range(TILES):
+                nc.vector.scalar_tensor_tensor(
+                    out=y[:, j, :],
+                    in0=y_psum[g, j // 2][:, j % 2, :],
+                    scalar=1.0,
+                    in1=bias2[:],
+                    op0=ALU.mult,
+                    op1=ALU.add,
+                    accum_out=total[:, j : j + 1],
+                )
+            y_rows[g], sums[g] = y, total
+
+        def spread(g):
+            square = work.tile([P, TILES], F32, name="square")
+            for j in range(TILES):
+                junk = work.tile([P, H], BF16, name="junk")
+                nc.scalar.activation(
+                    out=junk[:],
+                    in_=y_rows[g][:, j, :],
+                    func=ACT.Square,
+                    scale=-256.0,
+                    bias=sums[g][:, j : j + 1],
+                    accum_out=square[:, j : j + 1],
+                )
+            mean = work.tile([P, TILES], F32, name="mean")
+            var = work.tile([P, TILES], F32, name="var")
+            rstd = work.tile([P, TILES], F32, name="rstd")
+            nc.gpsimd.tensor_scalar(out=mean[:], in0=sums[g][:], scalar1=1.0 / H, scalar2=0.0, op0=ALU.mult, op1=ALU.add)
+            nc.gpsimd.tensor_scalar(out=var[:], in0=square[:], scalar1=2.0**-24, scalar2=EPS, op0=ALU.mult, op1=ALU.add)
+            nc.gpsimd.tensor_tensor(out=rstd[:], in0=var[:], in1=neg_half[:], op=ALU.pow)
+            stats[g] = mean, rstd
+
+        def normalize(g):
+            mean, rstd = stats.pop(g)
+            res = work.tile([P, TILES, H], F32, name="res")
+            for j in range(TILES):
+                nc.vector.scalar_tensor_tensor(
+                    out=y_rows[g][:, j, :], in0=y_rows[g][:, j, :], scalar=mean[:, j : j + 1], in1=gain[:], op0=ALU.subtract, op1=ALU.mult
+                )
+            for j in range(TILES):
+                nc.vector.scalar_tensor_tensor(
+                    out=res[:, j, :], in0=y_rows[g][:, j, :], scalar=rstd[:, j : j + 1], in1=shift[:], op0=ALU.mult, op1=ALU.add
+                )
+            nc.sync.dma_start(out=out_rows[g // 2, g % 2], in_=res[:].rearrange("p j c -> p (j c)"))
+
+        def at(stage, g):
+            if 0 <= g < GROUPS:
+                stage(g)
+
+        product(0)
+        turn(0)
+        nc.vector.tensor_copy(out=w1[:].rearrange("p (t m) -> p t m", t=4), in_=w1_in[:].rearrange("p (m t) -> p t m", t=4))
+        nc.vector.tensor_copy(out=w1_sc[:].rearrange("p (t m) -> p t m", t=4), in_=w1_sc_in[:].rearrange("p (m t) -> p t m", t=4))
+        nc.gpsimd.tensor_copy(out=bias1[:], in_=bias1_bf[:])
+        empty_turned(0)
+        product(1)
+        quantize_c(0)
+        turn(1)
+        for i in range(GROUPS + 2):
+            at(quantize_h, i - 1)
+            at(layer1, i)
+            at(empty_turned, i + 1)
+            at(product, i + 2)
+            at(layer2, i - 1)
+            at(turn, i + 2)
+            at(hidden, i)
+            at(quantize_c, i + 1)
+            at(add_bias2, i - 1)
+            at(interleave_s, i)
+            at(spread, i - 1)
+            at(normalize, i - 2)
+            at(interleave_v, i)

@@ -24,7 +24,7 @@ GROUPS = TOKENS // GROUP
 EPS = 1e-5
 FLOPS = 2 * TOKENS * C * F + 2 * TOKENS * F * H
 
-S_TOKENS = 320
+S_TOKENS = 352
 
 
 def tile_spatialattentionlayer_pb_t_w8_kernel(
@@ -51,7 +51,7 @@ def tile_spatialattentionlayer_pb_t_w8_kernel(
         gain = keep.tile([P, H], BF16, name="gain")
         shift = keep.tile([P, H], BF16, name="shift")
         ident = keep.tile([P, P], F32, name="ident")
-        neg_half = keep.tile([P, TILES], F32, name="neg_half")
+        eps = keep.tile([P, 1], F32, name="eps")
         warm = keep.tile([P, 1], F32, name="warm")
         w1_in = keep.tile([P, F], U32, name="w1_in", align_bytes=64)
         w1 = keep.tile([P, F], U32, name="w1", align_bytes=64)
@@ -71,10 +71,10 @@ def tile_spatialattentionlayer_pb_t_w8_kernel(
 
         nc.vector.memset(w1_sc_in[:].bitcast(I32), 0)
         nc.vector.memset(w2_sc[:].bitcast(I32), 0)
-        nc.vector.memset(warm[:], 0.0)
-        nc.gpsimd.memset(neg_half[:], -0.5)
+        nc.vector.memset(warm[:], 1.0)
+        nc.gpsimd.memset(eps[:], EPS)
         make_identity(nc, ident[:])
-        nc.scalar.activation(out=warm[:], in_=warm[:], func=ACT.Relu)
+        nc.scalar.activation(out=warm[:], in_=warm[:], func=ACT.Abs_reciprocal_sqrt)
 
         nc.sync.dma_start(out=scale_row[:], in_=pq_scale.rearrange("a b c -> (a b c)").partition_broadcast(P))
         load_pq(0)
@@ -236,11 +236,9 @@ def tile_spatialattentionlayer_pb_t_w8_kernel(
                     accum_out=square[:, j : j + 1],
                 )
             mean = work.tile([P, TILES], F32, name="mean")
-            var = work.tile([P, TILES], F32, name="var")
             rstd = work.tile([P, TILES], F32, name="rstd")
-            nc.gpsimd.tensor_scalar(out=mean[:], in0=sums[g][:], scalar1=1.0 / H, scalar2=0.0, op0=ALU.mult, op1=ALU.add)
-            nc.gpsimd.tensor_scalar(out=var[:], in0=square[:], scalar1=2.0**-24, scalar2=EPS, op0=ALU.mult, op1=ALU.add)
-            nc.gpsimd.tensor_tensor(out=rstd[:], in0=var[:], in1=neg_half[:], op=ALU.pow)
+            nc.scalar.activation(out=mean[:], in_=sums[g][:], func=ACT.Copy, scale=1.0 / H)
+            nc.scalar.activation(out=rstd[:], in_=square[:], func=ACT.Abs_reciprocal_sqrt, scale=2.0**-24, bias=eps[:])
             stats[g] = mean, rstd
 
         def normalize(g):

@@ -24,7 +24,8 @@ GROUPS = TOKENS // GROUP
 EPS = 1e-5
 FLOPS = 2 * TOKENS * C * F + 2 * TOKENS * F * H
 
-S_TOKENS = 352
+PE_TOKENS = 256
+S_TOKENS = 128
 
 
 def tile_spatialattentionlayer_pb_t_w8_kernel(
@@ -36,7 +37,8 @@ def tile_spatialattentionlayer_pb_t_w8_kernel(
         inputs = ctx.enter_context(tc.tile_pool(name="inputs", bufs=1))
         work = ctx.enter_context(tc.tile_pool(name="work", bufs=3))
         psum_c = ctx.enter_context(tc.psum_pool(name="psum_c", bufs=2))
-        psum_h = ctx.enter_context(tc.psum_pool(name="psum_h", bufs=4))
+        psum_h = ctx.enter_context(tc.psum_pool(name="psum_h", bufs=3))
+        psum_i = ctx.enter_context(tc.psum_pool(name="psum_i", bufs=1))
         psum_y = ctx.enter_context(tc.psum_pool(name="psum_y", bufs=2))
         ctx.enter_context(tc.manual_schedule())
 
@@ -51,6 +53,7 @@ def tile_spatialattentionlayer_pb_t_w8_kernel(
         gain = keep.tile([P, H], BF16, name="gain")
         shift = keep.tile([P, H], BF16, name="shift")
         ident = keep.tile([P, P], F32, name="ident")
+        ident_bf = keep.tile([P, P], BF16, name="ident_bf")
         eps = keep.tile([P, 1], F32, name="eps")
         warm = keep.tile([P, 1], F32, name="warm")
         w1_in = keep.tile([P, F], U32, name="w1_in", align_bytes=64)
@@ -74,6 +77,7 @@ def tile_spatialattentionlayer_pb_t_w8_kernel(
         nc.vector.memset(warm[:], 1.0)
         nc.gpsimd.memset(eps[:], EPS)
         make_identity(nc, ident[:])
+        make_identity(nc, ident_bf[:])
         nc.scalar.activation(out=warm[:], in_=warm[:], func=ACT.Abs_reciprocal_sqrt)
 
         nc.sync.dma_start(out=scale_row[:], in_=pq_scale.rearrange("a b c -> (a b c)").partition_broadcast(P))
@@ -180,12 +184,28 @@ def tile_spatialattentionlayer_pb_t_w8_kernel(
             src = h_flat[g][:, :, lo:hi].rearrange("p t (c i) -> p c t i", i=4)
             return dst, src
 
+        i_psum = {}
+
+        def interleave_pe(g):
+            ip = psum_i.tile([P, PE_TOKENS * 4], BF16, name="ip")
+            for half in range(2):
+                n0 = half * P
+                nc.tensor.matmul(
+                    out=ip[:, half * 512 : half * 512 + 512],
+                    lhsT=ident_bf[:],
+                    rhs=h_flat[g][:, :, n0 : n0 + P].rearrange("p t n -> p n t"),
+                    start=True,
+                    stop=True,
+                )
+            i_psum[g] = ip
+
         def interleave_s(g):
-            dst, src = interleave_views(g, 0, S_TOKENS)
+            dst, src = interleave_views(g, PE_TOKENS, PE_TOKENS + S_TOKENS)
             nc.scalar.copy(out=dst, in_=src)
+            nc.scalar.copy(out=h_grouped[g][:, 0 : PE_TOKENS * 4], in_=i_psum.pop(g)[:])
 
         def interleave_v(g):
-            dst, src = interleave_views(g, S_TOKENS, GROUP)
+            dst, src = interleave_views(g, PE_TOKENS + S_TOKENS, GROUP)
             nc.vector.tensor_copy(out=dst, in_=src)
 
         def quantize_h(g):
@@ -267,17 +287,18 @@ def tile_spatialattentionlayer_pb_t_w8_kernel(
         product(1)
         quantize_c(0)
         turn(1)
-        for i in range(GROUPS + 2):
-            at(quantize_h, i - 1)
+        for i in range(GROUPS + 3):
             at(layer1, i)
             at(empty_turned, i + 1)
             at(product, i + 2)
-            at(layer2, i - 1)
             at(turn, i + 2)
+            at(interleave_v, i - 1)
             at(hidden, i)
+            at(add_bias2, i - 2)
+            at(quantize_h, i - 1)
+            at(layer2, i - 1)
             at(quantize_c, i + 1)
-            at(add_bias2, i - 1)
+            at(spread, i - 2)
+            at(interleave_pe, i)
             at(interleave_s, i)
-            at(spread, i - 1)
-            at(normalize, i - 2)
-            at(interleave_v, i)
+            at(normalize, i - 3)

@@ -25,7 +25,8 @@ EPS = 1e-5
 FLOPS = 2 * TOKENS * C * F + 2 * TOKENS * F * H
 
 PE_TOKENS = 256
-S_TOKENS = 128
+S_TOKENS = 96
+G_TILES = 2
 
 
 def tile_spatialattentionlayer_pb_t_w8_kernel(
@@ -36,22 +37,24 @@ def tile_spatialattentionlayer_pb_t_w8_kernel(
         keep = ctx.enter_context(tc.tile_pool(name="keep", bufs=1))
         inputs = ctx.enter_context(tc.tile_pool(name="inputs", bufs=1))
         work = ctx.enter_context(tc.tile_pool(name="work", bufs=3))
+        small = ctx.enter_context(tc.tile_pool(name="small", bufs=6))
         psum_c = ctx.enter_context(tc.psum_pool(name="psum_c", bufs=2))
-        psum_h = ctx.enter_context(tc.psum_pool(name="psum_h", bufs=3))
+        psum_h = ctx.enter_context(tc.psum_pool(name="psum_h", bufs=2))
         psum_i = ctx.enter_context(tc.psum_pool(name="psum_i", bufs=1))
+        psum_x = ctx.enter_context(tc.psum_pool(name="psum_x", bufs=1))
         psum_y = ctx.enter_context(tc.psum_pool(name="psum_y", bufs=2))
         ctx.enter_context(tc.manual_schedule())
 
         pq_rows = pq_bytes.rearrange("b n c -> (b n) c").rearrange("(s p j) c -> s p (j c)", p=P, j=2 * TILES)
         att_rows = attended.rearrange("b n c -> (b n) c").rearrange("(s p k j) c -> s k p j c", p=P, k=2, j=TILES)
-        out_rows = out.rearrange("b n c -> (b n) c").rearrange("(s p k j) c -> s k p (j c)", p=P, k=2, j=TILES)
+        out_rows = out.rearrange("b n c -> (b n) c").rearrange("(s p k j) c -> s k p j c", p=P, k=2, j=TILES)
 
         scale_row = keep.tile([P, H], F32, name="scale_row")
         bias1_bf = keep.tile([P, 4], BF16, name="bias1_bf")
         bias1 = keep.tile([P, 4], F32, name="bias1")
-        bias2 = keep.tile([P, H], BF16, name="bias2")
+        bias2_bf = [keep.tile([P, 1], BF16, name="bias2_bf%d" % c) for c in range(2)]
         gain = keep.tile([P, H], BF16, name="gain")
-        shift = keep.tile([P, H], BF16, name="shift")
+        shift = keep.tile([P, G_TILES, H], BF16, name="shift")
         ident = keep.tile([P, P], F32, name="ident")
         ident_bf = keep.tile([P, P], BF16, name="ident_bf")
         eps = keep.tile([P, 1], F32, name="eps")
@@ -88,61 +91,53 @@ def tile_spatialattentionlayer_pb_t_w8_kernel(
             nc.sync.dma_start(
                 out=w1_sc_in[32 * q : 32 * q + 4, :].bitcast(I32), in_=w1_scales[0, 4 * q : 4 * q + 4, :].bitcast(I32)
             )
+        nc.sync.dma_start(out=bias1_bf[:], in_=bf1.rearrange("(p t) -> p t", t=4))
+        load_att(1)
+        nc.sync.dma_start(out=w2[:].bitcast(I32), in_=w2_words[0].rearrange("p n t -> p (n t)").bitcast(I32))
         for q in range(4):
             nc.sync.dma_start(
                 out=w2_sc[32 * q : 32 * q + 4, :].bitcast(I32), in_=w2_scales[0, 4 * q : 4 * q + 4, :].bitcast(I32)
             )
-        nc.sync.dma_start(out=bias1_bf[:], in_=bf1.rearrange("(p t) -> p t", t=4))
-        load_att(1)
-        nc.sync.dma_start(out=w2[:].bitcast(I32), in_=w2_words[0].rearrange("p n t -> p (n t)").bitcast(I32))
-        nc.sync.dma_start(out=bias2[:], in_=bf2.partition_broadcast(P))
+        for c in range(2):
+            nc.sync.dma_start(out=bias2_bf[c][:], in_=bf2.rearrange("(c p o) -> c p o", c=2, o=1)[c])
+        load_pq(1)
+        load_att(2)
+        load_att(3)
         nc.sync.dma_start(out=gain[:], in_=ln_g.partition_broadcast(P))
-        nc.sync.dma_start(out=shift[:], in_=ln_b.partition_broadcast(P))
-        for s in range(1, GROUPS // 2):
+        nc.sync.dma_start(out=shift[:, 0, :], in_=ln_b.partition_broadcast(P))
+        for s in range(2, GROUPS // 2):
             load_pq(s)
             load_att(2 * s)
             load_att(2 * s + 1)
 
-        def product(g):
-            for j in range(TILES):
-                base = (g % 2 * TILES + j) * H
-                nc.vector.tensor_tensor(
-                    out=c_in[g][:, j, 0:H],
-                    in0=codes_in[g // 2][:, base : base + H].bitcast(FP8),
-                    in1=scale_row[:],
-                    op=ALU.mult,
-                )
+        c_turned, c_grouped, c_mx = {}, {}, {}
+        h_psum, h_flat, h_psum_grouped, h_grouped, h_mx = {}, {}, {}, {}, {}
+        x_psum, y_turned, y_psum, stats, rstd, centered, scaled = {}, {}, {}, {}, {}, {}, {}
 
-        turned = {}
-        c_mx = {}
-        h_psum = {}
-        h_flat = {}
-        h_mx = {}
-        y_psum = {}
-        y_rows = {}
-        sums = {}
-        squares = {}
-        stats = {}
+        def product(g, j):
+            base = (g % 2 * TILES + j) * H
+            nc.vector.tensor_tensor(
+                out=c_in[g][:, j, 0:H],
+                in0=codes_in[g // 2][:, base : base + H].bitcast(FP8),
+                in1=scale_row[:],
+                op=ALU.mult,
+            )
 
-        def turn(g):
+        def turn(g, half):
             words = c_in[g][:].bitcast(F32)
-            for half in range(2):
-                ct = psum_c.tile([P, 2, 2, P], F32, name="ct")
-                for jj in range(2):
-                    for u in range(2):
-                        nc.tensor.transpose(ct[:, jj, u, :], words[:, 2 * half + jj, u : C // 2 : 2], ident[:])
-                turned[g, half] = ct
+            ct = psum_c.tile([P, 2, 2, P], F32, name="ct")
+            for jj in range(2):
+                for u in range(2):
+                    nc.tensor.transpose(ct[:, jj, u, :], words[:, 2 * half + jj, u : C // 2 : 2], ident[:])
+            c_turned[g, half] = ct
 
-        c_grouped = {}
-
-        def empty_turned(g):
-            grouped = work.tile([P, GROUP * 4], BF16, name="c_grouped", align_bytes=64)
-            for half in range(2):
-                nc.scalar.copy(
-                    out=grouped[:, half * 1024 : half * 1024 + 1024].bitcast(F32).rearrange("p (j r u) -> p j r u", j=2, u=2),
-                    in_=turned.pop((g, half))[:].rearrange("p j u r -> p j r u"),
-                )
-            c_grouped[g] = grouped
+        def empty_turned(g, half):
+            if g not in c_grouped:
+                c_grouped[g] = work.tile([P, GROUP * 4], BF16, name="c_grouped", align_bytes=64)
+            nc.scalar.copy(
+                out=c_grouped[g][:, half * 1024 : half * 1024 + 1024].bitcast(F32).rearrange("p (j r u) -> p j r u", j=2, u=2),
+                in_=c_turned.pop((g, half))[:].rearrange("p j u r -> p j r u"),
+            )
 
         def quantize(grouped, name):
             codes = work.tile([P, GROUP], U32, name=name + "_codes", align_bytes=64)
@@ -153,38 +148,34 @@ def tile_spatialattentionlayer_pb_t_w8_kernel(
         def quantize_c(g):
             c_mx[g] = quantize(c_grouped.pop(g), "c")
 
-        def layer1(g):
-            codes, scales = c_mx.pop(g)
-            h_psum[g] = []
-            for t in range(4):
-                hp = psum_h.tile([P, GROUP], F32, name="hp")
-                nc.tensor.matmul_mx(
-                    out=hp[:],
-                    lhsT=w1[:, t * P : t * P + P].bitcast(FP8X4),
-                    lhsT_scale=w1_sc[:, t * P : t * P + P],
-                    rhs=codes[:].bitcast(FP8X4),
-                    rhs_scale=scales[:],
-                    start=True,
-                    stop=True,
-                )
-                h_psum[g].append(hp)
+        def layer1(g, t):
+            codes, scales = c_mx[g]
+            hp = psum_h.tile([P, GROUP], F32, name="hp")
+            nc.tensor.matmul_mx(
+                out=hp[:],
+                lhsT=w1[:, t * P : t * P + P].bitcast(FP8X4),
+                lhsT_scale=w1_sc[:, t * P : t * P + P],
+                rhs=codes[:].bitcast(FP8X4),
+                rhs_scale=scales[:],
+                start=True,
+                stop=True,
+            )
+            h_psum[g, t] = hp
 
-        def hidden(g):
-            planes = work.tile([P, 4, GROUP], BF16, name="h_flat")
-            for t in range(4):
-                nc.scalar.activation(out=planes[:, t, :], in_=h_psum[g][t][:], func=ACT.Relu, bias=bias1[:, t : t + 1])
-            h_flat[g] = planes
+        def hidden(g, t):
+            if g not in h_flat:
+                h_flat[g] = work.tile([P, 4, GROUP], BF16, name="h_flat")
+            nc.scalar.activation(out=h_flat[g][:, t, :], in_=h_psum.pop((g, t))[:], func=ACT.Relu, bias=bias1[:, t : t + 1])
 
-        h_grouped = {}
-
-        def interleave_views(g, lo, hi):
+        def grouped(g):
             if g not in h_grouped:
                 h_grouped[g] = work.tile([P, GROUP * 4], BF16, name="h_grouped", align_bytes=64)
-            dst = h_grouped[g][:, lo * 4 : hi * 4].rearrange("p (c i t) -> p c t i", i=4, t=4)
+            return h_grouped[g]
+
+        def interleave_views(g, lo, hi):
+            dst = grouped(g)[:, lo * 4 : hi * 4].rearrange("p (c i t) -> p c t i", i=4, t=4)
             src = h_flat[g][:, :, lo:hi].rearrange("p t (c i) -> p c t i", i=4)
             return dst, src
-
-        i_psum = {}
 
         def interleave_pe(g):
             ip = psum_i.tile([P, PE_TOKENS * 4], BF16, name="ip")
@@ -197,12 +188,14 @@ def tile_spatialattentionlayer_pb_t_w8_kernel(
                     start=True,
                     stop=True,
                 )
-            i_psum[g] = ip
+            h_psum_grouped[g] = ip
+
+        def empty_interleaved(g):
+            nc.scalar.copy(out=grouped(g)[:, 0 : PE_TOKENS * 4], in_=h_psum_grouped.pop(g)[:])
 
         def interleave_s(g):
             dst, src = interleave_views(g, PE_TOKENS, PE_TOKENS + S_TOKENS)
             nc.scalar.copy(out=dst, in_=src)
-            nc.scalar.copy(out=h_grouped[g][:, 0 : PE_TOKENS * 4], in_=i_psum.pop(g)[:])
 
         def interleave_v(g):
             dst, src = interleave_views(g, PE_TOKENS + S_TOKENS, GROUP)
@@ -211,94 +204,139 @@ def tile_spatialattentionlayer_pb_t_w8_kernel(
         def quantize_h(g):
             h_mx[g] = quantize(h_grouped.pop(g), "h")
 
-        def layer2(g):
-            codes, scales = h_mx.pop(g)
-            for half in range(2):
-                yp = psum_y.tile([P, 2, H], F32, name="yp")
-                for jj in range(2):
-                    cols = slice((2 * half + jj) * P, (2 * half + jj + 1) * P)
-                    nc.tensor.matmul_mx(
-                        out=yp[:, jj, :],
-                        lhsT=codes[:, cols].bitcast(FP8X4),
-                        lhsT_scale=scales[:, cols],
-                        rhs=w2[:].bitcast(FP8X4),
-                        rhs_scale=w2_sc[:],
-                        start=True,
-                        stop=True,
-                    )
-                y_psum[g, half] = yp
+        def layer2(g, c):
+            codes, scales = h_mx[g]
+            xp = psum_x.tile([P, GROUP], F32, name="xp")
+            nc.tensor.matmul_mx(
+                out=xp[:],
+                lhsT=w2[:, c * P : c * P + P].bitcast(FP8X4),
+                lhsT_scale=w2_sc[:, c * P : c * P + P],
+                rhs=codes[:].bitcast(FP8X4),
+                rhs_scale=scales[:],
+                start=True,
+                stop=True,
+            )
+            x_psum[g, c] = xp
 
-        def add_bias2(g):
-            y = work.tile([P, TILES, H], F32, name="y")
-            total = work.tile([P, TILES], F32, name="total")
-            for j in range(TILES):
-                nc.vector.scalar_tensor_tensor(
-                    out=y[:, j, :],
-                    in0=y_psum[g, j // 2][:, j % 2, :],
-                    scalar=1.0,
-                    in1=bias2[:],
-                    op0=ALU.mult,
-                    op1=ALU.add,
-                    accum_out=total[:, j : j + 1],
-                )
-            y_rows[g], sums[g] = y, total
+        def add_bias2(g, c):
+            if g not in y_turned:
+                y_turned[g] = work.tile([P, 2, GROUP], F32, name="y_turned")
+            nc.scalar.activation(out=y_turned[g][:, c, :], in_=x_psum.pop((g, c))[:], func=ACT.Identity, bias=bias2_bf[c][:])
 
-        def spread(g):
-            square = work.tile([P, TILES], F32, name="square")
-            for j in range(TILES):
-                junk = work.tile([P, H], BF16, name="junk")
-                nc.scalar.activation(
-                    out=junk[:],
-                    in_=y_rows[g][:, j, :],
-                    func=ACT.Square,
-                    scale=-256.0,
-                    bias=sums[g][:, j : j + 1],
-                    accum_out=square[:, j : j + 1],
-                )
-            mean = work.tile([P, TILES], F32, name="mean")
-            rstd = work.tile([P, TILES], F32, name="rstd")
-            nc.scalar.activation(out=mean[:], in_=sums[g][:], func=ACT.Copy, scale=1.0 / H)
-            nc.scalar.activation(out=rstd[:], in_=square[:], func=ACT.Abs_reciprocal_sqrt, scale=2.0**-24, bias=eps[:])
-            stats[g] = mean, rstd
+        def turn_back(g, half):
+            yp = psum_y.tile([P, 2, H], F32, name="yp")
+            for jj in range(2):
+                j = 2 * half + jj
+                for c in range(2):
+                    nc.tensor.transpose(yp[:, jj, c * P : c * P + P], y_turned[g][:, c, j * P : j * P + P], ident[:])
+            y_psum[g, half] = yp
 
-        def normalize(g):
-            mean, rstd = stats.pop(g)
-            res = work.tile([P, TILES, H], F32, name="res")
-            for j in range(TILES):
-                nc.vector.scalar_tensor_tensor(
-                    out=y_rows[g][:, j, :], in0=y_rows[g][:, j, :], scalar=mean[:, j : j + 1], in1=gain[:], op0=ALU.subtract, op1=ALU.mult
-                )
-            for j in range(TILES):
-                nc.vector.scalar_tensor_tensor(
-                    out=res[:, j, :], in0=y_rows[g][:, j, :], scalar=rstd[:, j : j + 1], in1=shift[:], op0=ALU.mult, op1=ALU.add
-                )
-            nc.sync.dma_start(out=out_rows[g // 2, g % 2], in_=res[:].rearrange("p j c -> p (j c)"))
+        def statistics(g, half):
+            if g not in stats:
+                stats[g] = small.tile([P, 12], F32, name="stats")
+            nc.vector.bn_stats(out=stats[g][:, half * 6 : half * 6 + 6], in_=y_psum[g, half][:].rearrange("p j c -> p c j"))
 
-        def at(stage, g):
+        def inverse_std(g):
+            rstd[g] = small.tile([P, TILES], F32, name="rstd")
+            nc.scalar.activation(
+                out=rstd[g][:], in_=stats[g][:, 2:12:3], func=ACT.Abs_reciprocal_sqrt, scale=1.0 / H, bias=eps[:]
+            )
+
+        def center(g, j):
+            if g not in centered:
+                centered[g] = (
+                    work.tile([P, G_TILES, H], F32, name="centered_g"),
+                    work.tile([P, TILES - G_TILES, H], F32, name="centered_v"),
+                )
+            nc.vector.scalar_tensor_tensor(
+                out=centered[g][j // 2][:, j % 2, :],
+                in0=y_psum[g, j // 2][:, j % 2, :],
+                scalar=stats[g][:, 3 * j + 1 : 3 * j + 2],
+                in1=gain[:],
+                op0=ALU.subtract,
+                op1=ALU.mult,
+            )
+
+        def finish(g, j):
+            if (g, 1) not in scaled:
+                scaled[g, 1] = work.tile([P, TILES - G_TILES, H], F32, name="result_v")
+            nc.vector.scalar_tensor_tensor(
+                out=scaled[g, 1][:, j % 2, :],
+                in0=centered[g][1][:, j % 2, :],
+                scalar=rstd[g][:, j : j + 1],
+                in1=shift[:, 0, :],
+                op0=ALU.mult,
+                op1=ALU.add,
+            )
+            count[g] = count.get(g, 0) + 1
+            if count[g] == TILES - G_TILES:
+                nc.sync.dma_start(out=out_rows[g // 2, g % 2][:, G_TILES:TILES, :], in_=scaled[g, 1][:])
+
+        count = {}
+
+        def scale_rows(g):
+            rows = centered[g][0]
+            for j in range(G_TILES):
+                nc.gpsimd.tensor_scalar(
+                    out=rows[:, j, :], in0=rows[:, j, :], scalar1=rstd[g][:, j : j + 1], scalar2=0.0, op0=ALU.mult, op1=ALU.add
+                )
+
+        def shift_rows(g):
+            result = work.tile([P, G_TILES, H], F32, name="result_g")
+            nc.gpsimd.tensor_tensor(out=result[:], in0=centered[g][0][:], in1=shift[:], op=ALU.add)
+            nc.sync.dma_start(out=out_rows[g // 2, g % 2][:, 0:G_TILES, :], in_=result[:])
+
+        def at(stage, g, *part):
             if 0 <= g < GROUPS:
-                stage(g)
+                stage(g, *part)
 
-        product(0)
-        turn(0)
-        nc.vector.tensor_copy(out=w1[:].rearrange("p (t m) -> p t m", t=4), in_=w1_in[:].rearrange("p (m t) -> p t m", t=4))
-        nc.vector.tensor_copy(out=w1_sc[:].rearrange("p (t m) -> p t m", t=4), in_=w1_sc_in[:].rearrange("p (m t) -> p t m", t=4))
-        nc.gpsimd.tensor_copy(out=bias1[:], in_=bias1_bf[:])
-        empty_turned(0)
-        product(1)
-        quantize_c(0)
-        turn(1)
-        for i in range(GROUPS + 3):
-            at(layer1, i)
-            at(empty_turned, i + 1)
-            at(product, i + 2)
-            at(turn, i + 2)
+        for i in range(-3, GROUPS + 4):
+            if i == -1:
+                nc.vector.tensor_copy(
+                    out=w1[:].rearrange("p (t m) -> p t m", t=4), in_=w1_in[:].rearrange("p (m t) -> p t m", t=4)
+                )
+                nc.gpsimd.tensor_copy(
+                    out=w1_sc[:].rearrange("p (t m) -> p t m", t=4), in_=w1_sc_in[:].rearrange("p (m t) -> p t m", t=4)
+                )
+                nc.gpsimd.tensor_copy(out=bias1[:], in_=bias1_bf[:])
+            if i == 1:
+                nc.gpsimd.tensor_copy(out=shift[:, 1, :], in_=shift[:, 0, :])
+            at(layer1, i, 0)
             at(interleave_v, i - 1)
-            at(hidden, i)
-            at(add_bias2, i - 2)
+            at(interleave_pe, i - 1)
+            at(center, i - 3, 1)
+            at(layer1, i, 1)
+            at(empty_interleaved, i - 1)
+            at(product, i + 2, 0)
+            at(scale_rows, i - 3)
+            at(turn_back, i - 2, 0)
+            at(empty_turned, i + 1, 0)
+            at(product, i + 2, 1)
+            at(shift_rows, i - 3)
+            at(turn, i + 2, 1)
+            at(hidden, i, 0)
+            at(finish, i - 4, 3)
+            at(hidden, i, 1)
+            at(center, i - 3, 2)
+            at(center, i - 3, 3)
             at(quantize_h, i - 1)
-            at(layer2, i - 1)
+            at(turn_back, i - 2, 1)
+            at(statistics, i - 2, 0)
+            at(layer1, i, 2)
+            at(statistics, i - 2, 1)
+            at(layer2, i - 1, 0)
+            at(hidden, i, 2)
             at(quantize_c, i + 1)
-            at(spread, i - 2)
-            at(interleave_pe, i)
+            at(layer1, i, 3)
+            at(add_bias2, i - 1, 0)
+            at(finish, i - 3, 2)
+            at(turn, i + 2, 0)
+            at(inverse_std, i - 2)
+            at(product, i + 3, 2)
+            at(layer2, i - 1, 1)
+            at(hidden, i, 3)
+            at(center, i - 2, 0)
+            at(empty_turned, i + 2, 1)
+            at(product, i + 3, 3)
+            at(add_bias2, i - 1, 1)
             at(interleave_s, i)
-            at(normalize, i - 3)

@@ -24,9 +24,7 @@ GROUPS = TOKENS // GROUP
 EPS = 1e-5
 FLOPS = 2 * TOKENS * C * F + 2 * TOKENS * F * H
 
-PE_TOKENS = 256
-S_TOKENS = 96
-G_TILES = 2
+S_TOKENS = 256
 
 
 def tile_spatialattentionlayer_pb_t_w8_kernel(
@@ -39,60 +37,69 @@ def tile_spatialattentionlayer_pb_t_w8_kernel(
         work = ctx.enter_context(tc.tile_pool(name="work", bufs=3))
         small = ctx.enter_context(tc.tile_pool(name="small", bufs=6))
         psum_c = ctx.enter_context(tc.psum_pool(name="psum_c", bufs=2))
-        psum_h = ctx.enter_context(tc.psum_pool(name="psum_h", bufs=2))
-        psum_i = ctx.enter_context(tc.psum_pool(name="psum_i", bufs=1))
+        psum_h = ctx.enter_context(tc.psum_pool(name="psum_h", bufs=3))
         psum_x = ctx.enter_context(tc.psum_pool(name="psum_x", bufs=1))
         psum_y = ctx.enter_context(tc.psum_pool(name="psum_y", bufs=2))
         ctx.enter_context(tc.manual_schedule())
 
         pq_rows = pq_bytes.rearrange("b n c -> (b n) c").rearrange("(s p j) c -> s p (j c)", p=P, j=2 * TILES)
-        att_rows = attended.rearrange("b n c -> (b n) c").rearrange("(s p k j) c -> s k p j c", p=P, k=2, j=TILES)
-        out_rows = out.rearrange("b n c -> (b n) c").rearrange("(s p k j) c -> s k p j c", p=P, k=2, j=TILES)
+        att_rows = attended.rearrange("b n c -> (b n) c").rearrange("(s p k h x) c -> s k h p x c", p=P, k=2, h=2, x=2)
+        out_rows = out.rearrange("b n c -> (b n) c").rearrange("(s p k j) c -> s k p (j c)", p=P, k=2, j=TILES)
 
-        scale_row = keep.tile([P, H], F32, name="scale_row")
+        scale_row = keep.tile([P, 2, H], F32, name="scale_row")
         bias1_bf = keep.tile([P, 4], BF16, name="bias1_bf")
         bias1 = keep.tile([P, 4], F32, name="bias1")
         bias2_bf = [keep.tile([P, 1], BF16, name="bias2_bf%d" % c) for c in range(2)]
         gain = keep.tile([P, H], BF16, name="gain")
-        shift = keep.tile([P, G_TILES, H], BF16, name="shift")
+        shift = keep.tile([P, H], BF16, name="shift")
         ident = keep.tile([P, P], F32, name="ident")
-        ident_bf = keep.tile([P, P], BF16, name="ident_bf")
         eps = keep.tile([P, 1], F32, name="eps")
         warm = keep.tile([P, 1], F32, name="warm")
-        w1_in = keep.tile([P, F], U32, name="w1_in", align_bytes=64)
-        w1 = keep.tile([P, F], U32, name="w1", align_bytes=64)
-        w1_sc_in = keep.tile([P, F], U8, name="w1_sc_in", align_bytes=64)
-        w1_sc = keep.tile([P, F], U8, name="w1_sc", align_bytes=64)
+        w1_in = keep.tile([P, 2, F], U32, name="w1_in", align_bytes=64)
+        w1 = keep.tile([P, 2, F], U32, name="w1", align_bytes=64)
+        w1_sc_in = keep.tile([P, 2, F], U8, name="w1_sc_in", align_bytes=64)
+        w1_sc = keep.tile([P, 2, F], U8, name="w1_sc", align_bytes=64)
         w2 = keep.tile([P, H], U32, name="w2", align_bytes=64)
         w2_sc = keep.tile([P, H], U8, name="w2_sc", align_bytes=64)
 
         codes_in = [inputs.tile([P, 2 * TILES * H], U8, name="pq%d" % s) for s in range(GROUPS // 2)]
-        c_in = [inputs.tile([P, TILES, C], BF16, name="c%d" % g) for g in range(GROUPS)]
+        c_in = [inputs.tile([P, 2, 4, H], BF16, name="c%d" % g) for g in range(GROUPS)]
 
         def load_pq(s):
             nc.sync.dma_start(out=codes_in[s][:], in_=pq_rows[s])
 
-        def load_att(g):
-            nc.sync.dma_start(out=c_in[g][:, :, H:C], in_=att_rows[g // 2, g % 2])
+        def load_first_pq(k):
+            half = slice(k * TILES * H, (k + 1) * TILES * H)
+            nc.sync.dma_start(out=codes_in[0][:, half], in_=pq_rows[0][:, half])
+            load_att(k)
 
-        nc.vector.memset(w1_sc_in[:].bitcast(I32), 0)
+        def load_att(g):
+            for half in range(2):
+                nc.sync.dma_start(out=c_in[g][:, half, 0:4:3, :], in_=att_rows[g // 2, g % 2, half])
+
+        nc.vector.memset(w1_sc_in[:].rearrange("p s n -> p (s n)").bitcast(I32), 0)
         nc.vector.memset(w2_sc[:].bitcast(I32), 0)
         nc.vector.memset(warm[:], 1.0)
         nc.gpsimd.memset(eps[:], EPS)
         make_identity(nc, ident[:])
-        make_identity(nc, ident_bf[:])
         nc.scalar.activation(out=warm[:], in_=warm[:], func=ACT.Abs_reciprocal_sqrt)
 
-        nc.sync.dma_start(out=scale_row[:], in_=pq_scale.rearrange("a b c -> (a b c)").partition_broadcast(P))
-        load_pq(0)
-        load_att(0)
-        nc.sync.dma_start(out=w1_in[:].bitcast(I32), in_=w1_words[0].rearrange("p n t -> p (n t)").bitcast(I32))
-        for q in range(4):
-            nc.sync.dma_start(
-                out=w1_sc_in[32 * q : 32 * q + 4, :].bitcast(I32), in_=w1_scales[0, 4 * q : 4 * q + 4, :].bitcast(I32)
-            )
+        nc.sync.dma_start(out=scale_row[:, 0, :], in_=pq_scale.rearrange("a b c -> (a b c)").partition_broadcast(P))
+        load_first_pq(0)
+        nc.scalar.copy(out=scale_row[:, 1, :], in_=scale_row[:, 0, :])
+        load_first_pq(1)
+        w1_rows = w1_words[0].rearrange("p n t -> p (n t)").bitcast(I32)
+        for s in range(2):
+            nc.sync.dma_start(out=w1_in[64 * s : 64 * s + 64, 0, :].bitcast(I32), in_=w1_rows[64 - 64 * s : 128 - 64 * s, :])
+        nc.sync.dma_start(out=w1_in[:, 1, :].bitcast(I32), in_=w1_rows)
+        for s in range(2):
+            for q in range(4):
+                row = 4 * ((q + 2 - 2 * s) % 4)
+                nc.sync.dma_start(
+                    out=w1_sc_in[32 * q : 32 * q + 4, s, :].bitcast(I32), in_=w1_scales[0, row : row + 4, :].bitcast(I32)
+                )
         nc.sync.dma_start(out=bias1_bf[:], in_=bf1.rearrange("(p t) -> p t", t=4))
-        load_att(1)
+        load_pq(1)
         nc.sync.dma_start(out=w2[:].bitcast(I32), in_=w2_words[0].rearrange("p n t -> p (n t)").bitcast(I32))
         for q in range(4):
             nc.sync.dma_start(
@@ -100,42 +107,44 @@ def tile_spatialattentionlayer_pb_t_w8_kernel(
             )
         for c in range(2):
             nc.sync.dma_start(out=bias2_bf[c][:], in_=bf2.rearrange("(c p o) -> c p o", c=2, o=1)[c])
-        load_pq(1)
         load_att(2)
+        load_pq(2)
         load_att(3)
         nc.sync.dma_start(out=gain[:], in_=ln_g.partition_broadcast(P))
-        nc.sync.dma_start(out=shift[:, 0, :], in_=ln_b.partition_broadcast(P))
+        nc.sync.dma_start(out=shift[:], in_=ln_b.partition_broadcast(P))
         for s in range(2, GROUPS // 2):
-            load_pq(s)
             load_att(2 * s)
+            if s + 1 < GROUPS // 2:
+                load_pq(s + 1)
             load_att(2 * s + 1)
 
         c_turned, c_grouped, c_mx = {}, {}, {}
-        h_psum, h_flat, h_psum_grouped, h_grouped, h_mx = {}, {}, {}, {}, {}
-        x_psum, y_turned, y_psum, stats, rstd, centered, scaled = {}, {}, {}, {}, {}, {}, {}
+        h_psum, h_flat, h_grouped, h_mx = {}, {}, {}, {}
+        x_psum, y_turned, y_psum, stats, rstd, centered, result = {}, {}, {}, {}, {}, {}, {}
 
-        def product(g, j):
-            base = (g % 2 * TILES + j) * H
+        def product(g, half):
+            base = (g % 2 * TILES + 2 * half) * H
             nc.vector.tensor_tensor(
-                out=c_in[g][:, j, 0:H],
-                in0=codes_in[g // 2][:, base : base + H].bitcast(FP8),
-                in1=scale_row[:],
+                out=c_in[g][:, half, 1:3, :].rearrange("p x c -> p (x c)"),
+                in0=codes_in[g // 2][:, base : base + 2 * H].bitcast(FP8),
+                in1=scale_row[:].rearrange("p x c -> p (x c)"),
                 op=ALU.mult,
             )
 
         def turn(g, half):
-            words = c_in[g][:].bitcast(F32)
+            words = c_in[g][:].rearrange("p h x c -> p (h x c)").bitcast(F32)
             ct = psum_c.tile([P, 2, 2, P], F32, name="ct")
             for jj in range(2):
+                base = (2 * half + jj) * (C // 2)
                 for u in range(2):
-                    nc.tensor.transpose(ct[:, jj, u, :], words[:, 2 * half + jj, u : C // 2 : 2], ident[:])
+                    nc.tensor.transpose(ct[:, jj, u, :], words[:, base + u : base + C // 2 : 2], ident[:])
             c_turned[g, half] = ct
 
         def empty_turned(g, half):
             if g not in c_grouped:
                 c_grouped[g] = work.tile([P, GROUP * 4], BF16, name="c_grouped", align_bytes=64)
             nc.scalar.copy(
-                out=c_grouped[g][:, half * 1024 : half * 1024 + 1024].bitcast(F32).rearrange("p (j r u) -> p j r u", j=2, u=2),
+                out=c_grouped[g][:].bitcast(F32).rearrange("p (j h r u) -> p h j r u", j=2, h=2, u=2)[:, half],
                 in_=c_turned.pop((g, half))[:].rearrange("p j u r -> p j r u"),
             )
 
@@ -151,15 +160,17 @@ def tile_spatialattentionlayer_pb_t_w8_kernel(
         def layer1(g, t):
             codes, scales = c_mx[g]
             hp = psum_h.tile([P, GROUP], F32, name="hp")
-            nc.tensor.matmul_mx(
-                out=hp[:],
-                lhsT=w1[:, t * P : t * P + P].bitcast(FP8X4),
-                lhsT_scale=w1_sc[:, t * P : t * P + P],
-                rhs=codes[:].bitcast(FP8X4),
-                rhs_scale=scales[:],
-                start=True,
-                stop=True,
-            )
+            for s in range(2):
+                cols = slice(s * 2 * P, s * 2 * P + 2 * P)
+                nc.tensor.matmul_mx(
+                    out=hp[:, cols],
+                    lhsT=w1[:, s, t * P : t * P + P].bitcast(FP8X4),
+                    lhsT_scale=w1_sc[:, s, t * P : t * P + P],
+                    rhs=codes[:, cols].bitcast(FP8X4),
+                    rhs_scale=scales[:, cols],
+                    start=True,
+                    stop=True,
+                )
             h_psum[g, t] = hp
 
         def hidden(g, t):
@@ -172,34 +183,21 @@ def tile_spatialattentionlayer_pb_t_w8_kernel(
                 h_grouped[g] = work.tile([P, GROUP * 4], BF16, name="h_grouped", align_bytes=64)
             return h_grouped[g]
 
-        def interleave_views(g, lo, hi):
-            dst = grouped(g)[:, lo * 4 : hi * 4].rearrange("p (c i t) -> p c t i", i=4, t=4)
-            src = h_flat[g][:, :, lo:hi].rearrange("p t (c i) -> p c t i", i=4)
-            return dst, src
-
-        def interleave_pe(g):
-            ip = psum_i.tile([P, PE_TOKENS * 4], BF16, name="ip")
-            for half in range(2):
-                n0 = half * P
-                nc.tensor.matmul(
-                    out=ip[:, half * 512 : half * 512 + 512],
-                    lhsT=ident_bf[:],
-                    rhs=h_flat[g][:, :, n0 : n0 + P].rearrange("p t n -> p n t"),
-                    start=True,
-                    stop=True,
-                )
-            h_psum_grouped[g] = ip
-
-        def empty_interleaved(g):
-            nc.scalar.copy(out=grouped(g)[:, 0 : PE_TOKENS * 4], in_=h_psum_grouped.pop(g)[:])
-
         def interleave_s(g):
-            dst, src = interleave_views(g, PE_TOKENS, PE_TOKENS + S_TOKENS)
-            nc.scalar.copy(out=dst, in_=src)
+            nc.scalar.copy(
+                out=grouped(g)[:, 0 : S_TOKENS * 4].rearrange("p (c i t) -> p c t i", i=4, t=4),
+                in_=h_flat[g][:, :, 0:S_TOKENS].rearrange("p t (c i) -> p c t i", i=4),
+            )
 
-        def interleave_v(g):
-            dst, src = interleave_views(g, PE_TOKENS + S_TOKENS, GROUP)
-            nc.vector.tensor_copy(out=dst, in_=src)
+        def interleave_g(g):
+            nc.gpsimd.tensor_scalar(
+                out=grouped(g)[:, S_TOKENS * 4 :].rearrange("p (n t) -> p n t", t=4),
+                in0=h_flat[g][:, :, S_TOKENS:].rearrange("p t n -> p n t"),
+                scalar1=1.0,
+                scalar2=0.0,
+                op0=ALU.mult,
+                op1=ALU.add,
+            )
 
         def quantize_h(g):
             h_mx[g] = quantize(h_grouped.pop(g), "h")
@@ -242,101 +240,92 @@ def tile_spatialattentionlayer_pb_t_w8_kernel(
                 out=rstd[g][:], in_=stats[g][:, 2:12:3], func=ACT.Abs_reciprocal_sqrt, scale=1.0 / H, bias=eps[:]
             )
 
-        def center(g, j):
+        def center(g, q):
             if g not in centered:
-                centered[g] = (
-                    work.tile([P, G_TILES, H], F32, name="centered_g"),
-                    work.tile([P, TILES - G_TILES, H], F32, name="centered_v"),
-                )
+                centered[g] = work.tile([P, TILES, H], F32, name="centered")
             nc.vector.scalar_tensor_tensor(
-                out=centered[g][j // 2][:, j % 2, :],
-                in0=y_psum[g, j // 2][:, j % 2, :],
-                scalar=stats[g][:, 3 * j + 1 : 3 * j + 2],
+                out=centered[g][:, q, :],
+                in0=y_psum[g, q // 2][:, q % 2, :],
+                scalar=stats[g][:, 3 * q + 1 : 3 * q + 2],
                 in1=gain[:],
                 op0=ALU.subtract,
                 op1=ALU.mult,
             )
 
-        def finish(g, j):
-            if (g, 1) not in scaled:
-                scaled[g, 1] = work.tile([P, TILES - G_TILES, H], F32, name="result_v")
+        def finish(g, q):
+            if g not in result:
+                result[g] = work.tile([P, TILES, H], F32, name="result"), []
+            rows, done = result[g]
             nc.vector.scalar_tensor_tensor(
-                out=scaled[g, 1][:, j % 2, :],
-                in0=centered[g][1][:, j % 2, :],
-                scalar=rstd[g][:, j : j + 1],
-                in1=shift[:, 0, :],
+                out=rows[:, q % 2 * 2 + q // 2, :],
+                in0=centered[g][:, q, :],
+                scalar=rstd[g][:, q : q + 1],
+                in1=shift[:],
                 op0=ALU.mult,
                 op1=ALU.add,
             )
-            count[g] = count.get(g, 0) + 1
-            if count[g] == TILES - G_TILES:
-                nc.sync.dma_start(out=out_rows[g // 2, g % 2][:, G_TILES:TILES, :], in_=scaled[g, 1][:])
+            done.append(q)
+            j = q % 2 * 2 + q // 2
+            if g == GROUPS - 1:
+                nc.sync.dma_start(out=out_rows[g // 2, g % 2][:, j * H : j * H + H], in_=rows[:, j, :])
+            elif len(done) == TILES:
+                nc.sync.dma_start(out=out_rows[g // 2, g % 2], in_=rows[:].rearrange("p j c -> p (j c)"))
 
-        count = {}
-
-        def scale_rows(g):
-            rows = centered[g][0]
-            for j in range(G_TILES):
-                nc.gpsimd.tensor_scalar(
-                    out=rows[:, j, :], in0=rows[:, j, :], scalar1=rstd[g][:, j : j + 1], scalar2=0.0, op0=ALU.mult, op1=ALU.add
-                )
-
-        def shift_rows(g):
-            result = work.tile([P, G_TILES, H], F32, name="result_g")
-            nc.gpsimd.tensor_tensor(out=result[:], in0=centered[g][0][:], in1=shift[:], op=ALU.add)
-            nc.sync.dma_start(out=out_rows[g // 2, g % 2][:, 0:G_TILES, :], in_=result[:])
+        def products_done(i):
+            if i < -4:
+                return 0
+            return min(GROUPS, i + 7, max(i + 5, 2 * i + 7))
 
         def at(stage, g, *part):
             if 0 <= g < GROUPS:
                 stage(g, *part)
 
-        for i in range(-3, GROUPS + 4):
-            if i == -1:
-                nc.vector.tensor_copy(
-                    out=w1[:].rearrange("p (t m) -> p t m", t=4), in_=w1_in[:].rearrange("p (m t) -> p t m", t=4)
-                )
-                nc.gpsimd.tensor_copy(
-                    out=w1_sc[:].rearrange("p (t m) -> p t m", t=4), in_=w1_sc_in[:].rearrange("p (m t) -> p t m", t=4)
-                )
+        for i in range(-4, GROUPS + 2):
+            if i == -2:
+                for s in range(2):
+                    nc.vector.tensor_copy(
+                        out=w1[:, s, :].rearrange("p (t m) -> p t m", t=4), in_=w1_in[:, s, :].rearrange("p (m t) -> p t m", t=4)
+                    )
+                    engine = (nc.vector, nc.gpsimd)[s]
+                    engine.tensor_copy(
+                        out=w1_sc[:, s, :].rearrange("p (t m) -> p t m", t=4),
+                        in_=w1_sc_in[:, s, :].rearrange("p (m t) -> p t m", t=4),
+                    )
                 nc.gpsimd.tensor_copy(out=bias1[:], in_=bias1_bf[:])
-            if i == 1:
-                nc.gpsimd.tensor_copy(out=shift[:, 1, :], in_=shift[:, 0, :])
-            at(layer1, i, 0)
-            at(interleave_v, i - 1)
-            at(interleave_pe, i - 1)
-            at(center, i - 3, 1)
-            at(layer1, i, 1)
-            at(empty_interleaved, i - 1)
-            at(product, i + 2, 0)
-            at(scale_rows, i - 3)
-            at(turn_back, i - 2, 0)
-            at(empty_turned, i + 1, 0)
-            at(product, i + 2, 1)
-            at(shift_rows, i - 3)
-            at(turn, i + 2, 1)
-            at(hidden, i, 0)
-            at(finish, i - 4, 3)
-            at(hidden, i, 1)
-            at(center, i - 3, 2)
-            at(center, i - 3, 3)
-            at(quantize_h, i - 1)
-            at(turn_back, i - 2, 1)
-            at(statistics, i - 2, 0)
-            at(layer1, i, 2)
-            at(statistics, i - 2, 1)
-            at(layer2, i - 1, 0)
-            at(hidden, i, 2)
-            at(quantize_c, i + 1)
-            at(layer1, i, 3)
-            at(add_bias2, i - 1, 0)
-            at(finish, i - 3, 2)
-            at(turn, i + 2, 0)
-            at(inverse_std, i - 2)
-            at(product, i + 3, 2)
-            at(layer2, i - 1, 1)
-            at(hidden, i, 3)
+            for g in range(products_done(i - 1), products_done(i)):
+                product(g, 1)
+            at(layer1, i + 1, 0)
+            at(empty_turned, i + 3, 1)
+            at(center, i - 2, 1)
+            at(layer1, i + 1, 2)
+            at(hidden, i + 1, 0)
             at(center, i - 2, 0)
-            at(empty_turned, i + 2, 1)
-            at(product, i + 3, 3)
-            at(add_bias2, i - 1, 1)
-            at(interleave_s, i)
+            at(hidden, i + 1, 2)
+            at(center, i - 2, 2)
+            at(turn_back, i - 1, 0)
+            at(center, i - 2, 3)
+            at(finish, i - 2, 0)
+            at(turn_back, i - 1, 1)
+            at(quantize_h, i)
+            at(layer1, i + 1, 1)
+            at(finish, i - 2, 3)
+            at(layer2, i, 0)
+            at(hidden, i + 1, 1)
+            at(statistics, i - 1, 0)
+            at(layer1, i + 1, 3)
+            at(add_bias2, i, 0)
+            at(statistics, i - 1, 1)
+            at(turn, i + 3, 0)
+            at(hidden, i + 1, 3)
+            at(finish, i - 2, 2)
+            at(layer2, i, 1)
+            at(inverse_std, i - 1)
+            at(interleave_g, i + 1)
+            for g in range(products_done(i - 1), products_done(i)):
+                product(g, 0)
+            at(turn, i + 4, 1)
+            at(empty_turned, i + 3, 0)
+            at(quantize_c, i + 2)
+            at(add_bias2, i, 1)
+            at(finish, i - 2, 1)
+            at(interleave_s, i + 1)

from contextlib import ExitStack

import concourse.mybir as mybir
from concourse.masks import make_identity

F32 = mybir.dt.float32
BF16 = mybir.dt.bfloat16
I32 = mybir.dt.int32
U32 = mybir.dt.uint32
U8 = mybir.dt.uint8
FP8 = mybir.dt.float8_e4m3fn
FP8X4 = mybir.dt.float8_e4m3fn_x4
ALU = mybir.AluOpType
ACT = mybir.ActivationFunctionType

P = 128
H = 256
C = 512
F = 512
TOKENS = 8192
TILES = 4
GROUP = P * TILES
GROUPS = TOKENS // GROUP
EPS = 1e-5
FLOPS = 2 * TOKENS * C * F + 2 * TOKENS * F * H

S_TOKENS = 256


def tile_spatialattentionlayer_pb_t_w8_kernel(
    tc, pq_bytes, pq_scale, attended, w1_words, w1_scales, bf1, w2_words, w2_scales, bf2, ln_g, ln_b, out
):
    nc = tc.nc
    with ExitStack() as ctx:
        keep = ctx.enter_context(tc.tile_pool(name="keep", bufs=1))
        inputs = ctx.enter_context(tc.tile_pool(name="inputs", bufs=1))
        work = ctx.enter_context(tc.tile_pool(name="work", bufs=3))
        small = ctx.enter_context(tc.tile_pool(name="small", bufs=6))
        psum_c = ctx.enter_context(tc.psum_pool(name="psum_c", bufs=2))
        psum_h = ctx.enter_context(tc.psum_pool(name="psum_h", bufs=3))
        psum_x = ctx.enter_context(tc.psum_pool(name="psum_x", bufs=1))
        psum_y = ctx.enter_context(tc.psum_pool(name="psum_y", bufs=2))
        ctx.enter_context(tc.manual_schedule())

        pq_rows = pq_bytes.rearrange("b n c -> (b n) c").rearrange("(s p j) c -> s p (j c)", p=P, j=2 * TILES)
        att_rows = attended.rearrange("b n c -> (b n) c").rearrange("(s p k h x) c -> s k h p x c", p=P, k=2, h=2, x=2)
        out_rows = out.rearrange("b n c -> (b n) c").rearrange("(s p k j) c -> s k p (j c)", p=P, k=2, j=TILES)

        scale_row = keep.tile([P, 2, H], F32, name="scale_row")
        bias1_bf = keep.tile([P, 4], BF16, name="bias1_bf")
        bias1 = keep.tile([P, 4], F32, name="bias1")
        bias2_bf = [keep.tile([P, 1], BF16, name="bias2_bf%d" % c) for c in range(2)]
        gain = keep.tile([P, H], BF16, name="gain")
        shift = keep.tile([P, H], BF16, name="shift")
        ident = keep.tile([P, P], F32, name="ident")
        eps = keep.tile([P, 1], F32, name="eps")
        warm = keep.tile([P, 1], F32, name="warm")
        w1_in = keep.tile([P, 2, F], U32, name="w1_in", align_bytes=64)
        w1 = keep.tile([P, 2, F], U32, name="w1", align_bytes=64)
        w1_sc_in = keep.tile([P, 2, F], U8, name="w1_sc_in", align_bytes=64)
        w1_sc = keep.tile([P, 2, F], U8, name="w1_sc", align_bytes=64)
        w2 = keep.tile([P, H], U32, name="w2", align_bytes=64)
        w2_sc = keep.tile([P, H], U8, name="w2_sc", align_bytes=64)

        codes_in = [inputs.tile([P, 2 * TILES * H], U8, name="pq%d" % s) for s in range(GROUPS // 2)]
        c_in = [inputs.tile([P, 2, 4, H], BF16, name="c%d" % g) for g in range(GROUPS)]

        def load_pq(s):
            nc.sync.dma_start(out=codes_in[s][:], in_=pq_rows[s])

        def load_first_pq(k):
            half = slice(k * TILES * H, (k + 1) * TILES * H)
            nc.sync.dma_start(out=codes_in[0][:, half], in_=pq_rows[0][:, half])
            load_att(k)

        def load_att(g):
            for half in range(2):
                nc.sync.dma_start(out=c_in[g][:, half, 0:4:3, :], in_=att_rows[g // 2, g % 2, half])

        nc.vector.memset(w1_sc_in[:].rearrange("p s n -> p (s n)").bitcast(I32), 0)
        nc.vector.memset(w2_sc[:].bitcast(I32), 0)
        nc.vector.memset(warm[:], 1.0)
        nc.gpsimd.memset(eps[:], EPS)
        make_identity(nc, ident[:])
        nc.scalar.activation(out=warm[:], in_=warm[:], func=ACT.Abs_reciprocal_sqrt)

        nc.sync.dma_start(out=scale_row[:, 0, :], in_=pq_scale.rearrange("a b c -> (a b c)").partition_broadcast(P))
        load_first_pq(0)
        nc.scalar.copy(out=scale_row[:, 1, :], in_=scale_row[:, 0, :])
        load_first_pq(1)
        w1_rows = w1_words[0].rearrange("p n t -> p (n t)").bitcast(I32)
        for s in range(2):
            nc.sync.dma_start(out=w1_in[64 * s : 64 * s + 64, 0, :].bitcast(I32), in_=w1_rows[64 - 64 * s : 128 - 64 * s, :])
        nc.sync.dma_start(out=w1_in[:, 1, :].bitcast(I32), in_=w1_rows)
        for s in range(2):
            for q in range(4):
                row = 4 * ((q + 2 - 2 * s) % 4)
                nc.sync.dma_start(
                    out=w1_sc_in[32 * q : 32 * q + 4, s, :].bitcast(I32), in_=w1_scales[0, row : row + 4, :].bitcast(I32)
                )
        nc.sync.dma_start(out=bias1_bf[:], in_=bf1.rearrange("(p t) -> p t", t=4))
        load_pq(1)
        nc.sync.dma_start(out=w2[:].bitcast(I32), in_=w2_words[0].rearrange("p n t -> p (n t)").bitcast(I32))
        for q in range(4):
            nc.sync.dma_start(
                out=w2_sc[32 * q : 32 * q + 4, :].bitcast(I32), in_=w2_scales[0, 4 * q : 4 * q + 4, :].bitcast(I32)
            )
        for c in range(2):
            nc.sync.dma_start(out=bias2_bf[c][:], in_=bf2.rearrange("(c p o) -> c p o", c=2, o=1)[c])
        load_att(2)
        load_pq(2)
        load_att(3)
        nc.sync.dma_start(out=gain[:], in_=ln_g.partition_broadcast(P))
        nc.sync.dma_start(out=shift[:], in_=ln_b.partition_broadcast(P))
        for s in range(2, GROUPS // 2):
            load_att(2 * s)
            if s + 1 < GROUPS // 2:
                load_pq(s + 1)
            load_att(2 * s + 1)

        c_turned, c_grouped, c_mx = {}, {}, {}
        h_psum, h_flat, h_grouped, h_mx = {}, {}, {}, {}
        x_psum, y_turned, y_psum, stats, rstd, centered, result = {}, {}, {}, {}, {}, {}, {}

        def product(g, half):
            base = (g % 2 * TILES + 2 * half) * H
            nc.vector.tensor_tensor(
                out=c_in[g][:, half, 1:3, :].rearrange("p x c -> p (x c)"),
                in0=codes_in[g // 2][:, base : base + 2 * H].bitcast(FP8),
                in1=scale_row[:].rearrange("p x c -> p (x c)"),
                op=ALU.mult,
            )

        def turn(g, half):
            words = c_in[g][:].rearrange("p h x c -> p (h x c)").bitcast(F32)
            ct = psum_c.tile([P, 2, 2, P], F32, name="ct")
            for jj in range(2):
                base = (2 * half + jj) * (C // 2)
                for u in range(2):
                    nc.tensor.transpose(ct[:, jj, u, :], words[:, base + u : base + C // 2 : 2], ident[:])
            c_turned[g, half] = ct

        def empty_turned(g, half):
            if g not in c_grouped:
                c_grouped[g] = work.tile([P, GROUP * 4], BF16, name="c_grouped", align_bytes=64)
            nc.scalar.copy(
                out=c_grouped[g][:].bitcast(F32).rearrange("p (j h r u) -> p h j r u", j=2, h=2, u=2)[:, half],
                in_=c_turned.pop((g, half))[:].rearrange("p j u r -> p j r u"),
            )

        def quantize(grouped, name):
            codes = work.tile([P, GROUP], U32, name=name + "_codes", align_bytes=64)
            scales = work.tile([P, GROUP], U8, name=name + "_scales", align_bytes=64)
            nc.vector.quantize_mx(out=codes[:].bitcast(FP8X4), scales=scales[:], in_=grouped[:])
            return codes, scales

        def quantize_c(g):
            c_mx[g] = quantize(c_grouped.pop(g), "c")

        def layer1(g, t):
            codes, scales = c_mx[g]
            hp = psum_h.tile([P, GROUP], F32, name="hp")
            for s in range(2):
                cols = slice(s * 2 * P, s * 2 * P + 2 * P)
                nc.tensor.matmul_mx(
                    out=hp[:, cols],
                    lhsT=w1[:, s, t * P : t * P + P].bitcast(FP8X4),
                    lhsT_scale=w1_sc[:, s, t * P : t * P + P],
                    rhs=codes[:, cols].bitcast(FP8X4),
                    rhs_scale=scales[:, cols],
                    start=True,
                    stop=True,
                )
            h_psum[g, t] = hp

        def hidden(g, t):
            if g not in h_flat:
                h_flat[g] = work.tile([P, 4, GROUP], BF16, name="h_flat")
            nc.scalar.activation(out=h_flat[g][:, t, :], in_=h_psum.pop((g, t))[:], func=ACT.Relu, bias=bias1[:, t : t + 1])

        def grouped(g):
            if g not in h_grouped:
                h_grouped[g] = work.tile([P, GROUP * 4], BF16, name="h_grouped", align_bytes=64)
            return h_grouped[g]

        def interleave_s(g):
            nc.scalar.copy(
                out=grouped(g)[:, 0 : S_TOKENS * 4].rearrange("p (c i t) -> p c t i", i=4, t=4),
                in_=h_flat[g][:, :, 0:S_TOKENS].rearrange("p t (c i) -> p c t i", i=4),
            )

        def interleave_g(g):
            nc.gpsimd.tensor_scalar(
                out=grouped(g)[:, S_TOKENS * 4 :].rearrange("p (n t) -> p n t", t=4),
                in0=h_flat[g][:, :, S_TOKENS:].rearrange("p t n -> p n t"),
                scalar1=1.0,
                scalar2=0.0,
                op0=ALU.mult,
                op1=ALU.add,
            )

        def quantize_h(g):
            h_mx[g] = quantize(h_grouped.pop(g), "h")

        def layer2(g, c):
            codes, scales = h_mx[g]
            xp = psum_x.tile([P, GROUP], F32, name="xp")
            nc.tensor.matmul_mx(
                out=xp[:],
                lhsT=w2[:, c * P : c * P + P].bitcast(FP8X4),
                lhsT_scale=w2_sc[:, c * P : c * P + P],
                rhs=codes[:].bitcast(FP8X4),
                rhs_scale=scales[:],
                start=True,
                stop=True,
            )
            x_psum[g, c] = xp

        def add_bias2(g, c):
            if g not in y_turned:
                y_turned[g] = work.tile([P, 2, GROUP], F32, name="y_turned")
            nc.scalar.activation(out=y_turned[g][:, c, :], in_=x_psum.pop((g, c))[:], func=ACT.Identity, bias=bias2_bf[c][:])

        def turn_back(g, half):
            yp = psum_y.tile([P, 2, H], F32, name="yp")
            for jj in range(2):
                j = 2 * half + jj
                for c in range(2):
                    nc.tensor.transpose(yp[:, jj, c * P : c * P + P], y_turned[g][:, c, j * P : j * P + P], ident[:])
            y_psum[g, half] = yp

        def statistics(g, half):
            if g not in stats:
                stats[g] = small.tile([P, 12], F32, name="stats")
            nc.vector.bn_stats(out=stats[g][:, half * 6 : half * 6 + 6], in_=y_psum[g, half][:].rearrange("p j c -> p c j"))

        def inverse_std(g):
            rstd[g] = small.tile([P, TILES], F32, name="rstd")
            nc.scalar.activation(
                out=rstd[g][:], in_=stats[g][:, 2:12:3], func=ACT.Abs_reciprocal_sqrt, scale=1.0 / H, bias=eps[:]
            )

        def center(g, q):
            if g not in centered:
                centered[g] = work.tile([P, TILES, H], F32, name="centered")
            nc.vector.scalar_tensor_tensor(
                out=centered[g][:, q, :],
                in0=y_psum[g, q // 2][:, q % 2, :],
                scalar=stats[g][:, 3 * q + 1 : 3 * q + 2],
                in1=gain[:],
                op0=ALU.subtract,
                op1=ALU.mult,
            )

        def finish(g, q):
            if g not in result:
                result[g] = work.tile([P, TILES, H], F32, name="result"), []
            rows, done = result[g]
            nc.vector.scalar_tensor_tensor(
                out=rows[:, q % 2 * 2 + q // 2, :],
                in0=centered[g][:, q, :],
                scalar=rstd[g][:, q : q + 1],
                in1=shift[:],
                op0=ALU.mult,
                op1=ALU.add,
            )
            done.append(q)
            j = q % 2 * 2 + q // 2
            if g == GROUPS - 1:
                nc.sync.dma_start(out=out_rows[g // 2, g % 2][:, j * H : j * H + H], in_=rows[:, j, :])
            elif len(done) == TILES:
                nc.sync.dma_start(out=out_rows[g // 2, g % 2], in_=rows[:].rearrange("p j c -> p (j c)"))

        def products_done(i):
            if i < -4:
                return 0
            return min(GROUPS, i + 7, max(i + 5, 2 * i + 7))

        def at(stage, g, *part):
            if 0 <= g < GROUPS:
                stage(g, *part)

        for i in range(-4, GROUPS + 2):
            if i == -2:
                for s in range(2):
                    nc.vector.tensor_copy(
                        out=w1[:, s, :].rearrange("p (t m) -> p t m", t=4), in_=w1_in[:, s, :].rearrange("p (m t) -> p t m", t=4)
                    )
                    engine = (nc.vector, nc.gpsimd)[s]
                    engine.tensor_copy(
                        out=w1_sc[:, s, :].rearrange("p (t m) -> p t m", t=4),
                        in_=w1_sc_in[:, s, :].rearrange("p (m t) -> p t m", t=4),
                    )
                nc.gpsimd.tensor_copy(out=bias1[:], in_=bias1_bf[:])
            for g in range(products_done(i - 1), products_done(i)):
                product(g, 1)
            at(layer1, i + 1, 0)
            at(empty_turned, i + 3, 1)
            at(center, i - 2, 1)
            at(layer1, i + 1, 2)
            at(hidden, i + 1, 0)
            at(center, i - 2, 0)
            at(hidden, i + 1, 2)
            at(center, i - 2, 2)
            at(turn_back, i - 1, 0)
            at(center, i - 2, 3)
            at(finish, i - 2, 0)
            at(turn_back, i - 1, 1)
            at(quantize_h, i)
            at(layer1, i + 1, 1)
            at(finish, i - 2, 3)
            at(layer2, i, 0)
            at(hidden, i + 1, 1)
            at(statistics, i - 1, 0)
            at(layer1, i + 1, 3)
            at(add_bias2, i, 0)
            at(statistics, i - 1, 1)
            at(turn, i + 3, 0)
            at(hidden, i + 1, 3)
            at(finish, i - 2, 2)
            at(layer2, i, 1)
            at(inverse_std, i - 1)
            at(interleave_g, i + 1)
            for g in range(products_done(i - 1), products_done(i)):
                product(g, 0)
            at(turn, i + 4, 1)
            at(empty_turned, i + 3, 0)
            at(quantize_c, i + 2)
            at(add_bias2, i, 1)
            at(finish, i - 2, 1)
            at(interleave_s, i + 1)
